import numpy as np
import ml_dtypes


def mxq(x, axis, fmt="e4m3"):
    dtype, down = {"e4m3": (ml_dtypes.float8_e4m3fn, 7), "e5m2": (ml_dtypes.float8_e5m2, 14)}[fmt]
    v = np.moveaxis(np.asarray(x, np.float32).astype(ml_dtypes.bfloat16).astype(np.float64), axis, -1)
    blocks = v.reshape(v.shape[:-1] + (-1, 32))
    amax = np.abs(blocks).max(-1, keepdims=True)
    byte = np.maximum(np.where(amax > 0, np.frexp(amax)[1] - 1 + 127, 0) - down, 1)
    scale = np.exp2(byte - 127.0)
    codes = (blocks / scale).astype(np.float32).astype(dtype).astype(np.float64)
    return np.moveaxis((codes * scale).reshape(v.shape), -1, axis)


WIDE = False


def mx_kscale(k):
    if not WIDE:
        return np.ones(k)
    levels = np.array([10, -10, 5, -5, 0])
    a = np.random.permutation(np.resize(levels, k // 512 * 4)).reshape(k // 512, 4)
    idx = np.arange(k)
    return np.exp2(a[idx // 512, idx % 128 // 32])


BF16 = ml_dtypes.bfloat16


def bf(x):
    return np.asarray(x, np.float32).astype(BF16)


def f64(x):
    return np.asarray(x).astype(np.float64)


B, C, HH, WW, NH, HD, F = 4, 512, 16, 16, 8, 64, 2048
EPS = 1e-5


def layer_norm(v, w, b):
    mu = v.mean(-1, keepdims=True)
    var = ((v - mu) ** 2).mean(-1, keepdims=True)
    return (v - mu) * (1.0 / np.sqrt(var + EPS)) * w + b


def setup_inputs():
    s = mx_kscale(F)
    return {"h": bf(np.maximum(np.random.standard_normal((B, HH, WW, F)), 0.0) * 0.125 * s),
            "ffn2_w": bf(np.random.standard_normal((C, F)) * 0.5 / np.sqrt(F) / s),
            "ffn2_b": bf(np.random.standard_normal(C) * 0.02),
            "scale_ffn": bf(0.1 * (1.0 + 0.1 * np.random.standard_normal(1))),
            "ln2_w": bf(1.0 + 0.1 * np.random.standard_normal(C)),
            "ln2_b": bf(0.1 * np.random.standard_normal(C)),
            "scale_norm2": bf(1.5 * (1.0 + 0.1 * np.random.standard_normal(1))),
            "x": bf(np.random.standard_normal((B, C, HH, WW)))}


def reference(h, ffn2_w, ffn2_b, scale_ffn, ln2_w, ln2_b, scale_norm2, x):
    y2 = ((mxq(f64(h), 3, "e4m3") @ mxq(f64(ffn2_w), 1, "e4m3").T) + f64(ffn2_b)) * f64(scale_ffn)
    y2 = layer_norm(y2, f64(ln2_w), f64(ln2_b)) * f64(scale_norm2)
    out = np.maximum(y2 + f64(x).transpose(0, 2, 3, 1), 0.0)
    return out.transpose(0, 3, 1, 2)

@@ -1,0 +1,250 @@
+from contextlib import ExitStack
+
+import concourse.mybir as mybir
+from concourse.masks import make_identity
+
+F32 = mybir.dt.float32
+BF16 = mybir.dt.bfloat16
+U32 = mybir.dt.uint32
+U8 = mybir.dt.uint8
+FP8X4 = mybir.dt.float8_e4m3fn_x4
+ALU = mybir.AluOpType
+ACT = mybir.ActivationFunctionType
+
+P = 128
+K = 2048
+K_PASS = 512
+PASSES = K // K_PASS
+WORDS_PASS = K_PASS // 2
+CHANNELS = 512
+CH_BLOCKS = CHANNELS // P
+IMAGES = 4
+IMAGE_PIXELS = 256
+TILES = IMAGES * IMAGE_PIXELS // P
+TILES_IMAGE = IMAGE_PIXELS // P
+EPS = 1e-5
+
+FLOPS = 2 * IMAGES * IMAGE_PIXELS * CHANNELS * K
+
+
+def tile_transformerconvblock_pc_kernel(
+    tc, h, ffn2_w, ffn2_b, scale_ffn, ln2_w, ln2_b, scale_norm2, x, out
+):
+    nc = tc.nc
+
+    h_rows = h.rearrange("b i j k -> (b i j) k")
+    w_blocks = ffn2_w.rearrange("(r t) k -> r t k", t=CH_BLOCKS)
+    x_images = x.rearrange("b (r t) i j -> r b (t i j)", t=CH_BLOCKS)
+    out_images = out.rearrange("b (r t) i j -> r b (t i j)", t=CH_BLOCKS)
+
+    with ExitStack() as stack:
+        stack.enter_context(tc.manual_schedule())
+        const = stack.enter_context(tc.tile_pool(name="const", bufs=1))
+        raw = stack.enter_context(tc.tile_pool(name="raw", bufs=1))
+        front = stack.enter_context(tc.tile_pool(name="front", bufs=3))
+        back = stack.enter_context(tc.tile_pool(name="back", bufs=3))
+        small = stack.enter_context(tc.tile_pool(name="small", bufs=4))
+        image = stack.enter_context(tc.tile_pool(name="image", bufs=2))
+        psum = stack.enter_context(tc.psum_pool(name="psum", bufs=2))
+
+        vec_rows = const.tile([P, CHANNELS + 32], BF16)
+        nc.vector.memset(vec_rows[:], 0.0)
+        ones = const.tile([P, P], BF16)
+        nc.vector.memset(ones[:], 1.0)
+        nc.scalar.dma_start(out=vec_rows[0:1, 0:CHANNELS], in_=ffn2_b.rearrange("(o c) -> o c", o=1))
+        nc.scalar.dma_start(
+            out=vec_rows[0:1, CHANNELS : CHANNELS + 1], in_=scale_ffn.rearrange("(o c) -> o c", o=1)
+        )
+        nc.scalar.dma_start(
+            out=vec_rows[0:1, CHANNELS + 16 : CHANNELS + 17],
+            in_=scale_norm2.rearrange("(o c) -> o c", o=1),
+        )
+        gain_raw = const.tile([P, CH_BLOCKS], BF16)
+        nc.scalar.dma_start(out=gain_raw[:], in_=ln2_w.rearrange("(r t) -> r t", t=CH_BLOCKS))
+        shift_raw = const.tile([P, CH_BLOCKS], BF16)
+        nc.scalar.dma_start(out=shift_raw[:], in_=ln2_b.rearrange("(r t) -> r t", t=CH_BLOCKS))
+
+        warm = const.tile([P, 1], F32)
+        nc.scalar.sqrt(out=warm[:], in_=ones[:, 0:1])
+
+        w_raw = []
+        for t in range(CH_BLOCKS):
+            w_tile = raw.tile([P, K], BF16, name="w_raw%d" % t)
+            nc.sync.dma_start(out=w_tile[:], in_=w_blocks[:, t, :])
+            w_raw.append(w_tile)
+        h_raw = []
+        x_raw = []
+        for i in range(TILES):
+            h_tile = raw.tile([P, K], BF16, name="h_raw%d" % i)
+            nc.sync.dma_start(out=h_tile[:], in_=h_rows[i * P : (i + 1) * P, :])
+            h_raw.append(h_tile)
+            if i >= TILES_IMAGE and i % TILES_IMAGE == 1:
+                load_x(nc, raw, x_images, x_raw)
+        load_x(nc, raw, x_images, x_raw)
+
+        ident = const.tile([P, P], F32)
+        make_identity(nc, ident[:])
+
+        w_codes = const.tile([P, PASSES, CHANNELS], U32, align_bytes=64)
+        w_scales = const.tile([P, PASSES, CHANNELS], U8, align_bytes=64)
+        for t in range(CH_BLOCKS):
+            w_grouped = front.tile([P, PASSES * P * 4], BF16, tag="grouped", align_bytes=64)
+            k_to_partitions(nc, psum, w_raw[t], ident, w_grouped, (nc.scalar.copy, nc.vector.tensor_copy))
+            for g in range(PASSES):
+                nc.vector.quantize_mx(
+                    out=w_codes[:, g, t * P : (t + 1) * P].bitcast(FP8X4),
+                    scales=w_scales[:, g, t * P : (t + 1) * P],
+                    in_=w_grouped[:, g * P * 4 : (g + 1) * P * 4],
+                )
+
+        bias_ps = psum.tile([P, CHANNELS], F32, tag="acc")
+        nc.tensor.matmul(out=bias_ps[:], lhsT=ones[:], rhs=vec_rows[:, 0:CHANNELS], start=True, stop=True)
+        mult_ps = psum.tile([P, 32], F32, tag="acc")
+        nc.tensor.matmul(out=mult_ps[:], lhsT=ones[:], rhs=vec_rows[:, CHANNELS : CHANNELS + 32], start=True, stop=True)
+        bias_all = const.tile([P, CH_BLOCKS, P], F32)
+        nc.vector.tensor_copy(out=bias_all[:], in_=bias_ps[:].rearrange("p (r t) -> p t r", t=CH_BLOCKS))
+        mult = const.tile([P, 32], F32)
+        nc.vector.tensor_copy(out=mult[:], in_=mult_ps[:])
+        s_ffn = mult[:, 0:1]
+        s_norm = mult[:, 16:17]
+        s_ffn_sq = const.tile([P, 1], F32)
+        nc.vector.tensor_mul(out=s_ffn_sq[:], in0=s_ffn, in1=s_ffn)
+        gain = const.tile([P, CH_BLOCKS], F32)
+        nc.vector.tensor_scalar(
+            out=gain[:], in0=gain_raw[:], scalar1=s_norm, scalar2=s_ffn, op0=ALU.mult, op1=ALU.mult
+        )
+        shift = const.tile([P, CH_BLOCKS], F32)
+        nc.vector.tensor_scalar_mul(out=shift[:], in0=shift_raw[:], scalar1=s_norm)
+
+        grouped = {}
+        codes = {}
+        scales = {}
+        acc = {}
+        v = {}
+        moments = {}
+        std = {}
+        normed = {}
+        turned = {}
+
+        def transpose_h(i):
+            grouped[i] = front.tile([P, PASSES * P * 4], BF16, tag="grouped", name="h_grouped", align_bytes=64)
+            k_to_partitions(nc, psum, h_raw[i], ident, grouped[i], (nc.scalar.copy, nc.scalar.copy))
+
+        def quantise_h(i):
+            codes[i] = front.tile([P, PASSES * P], U32, tag="codes", name="h_codes", align_bytes=64)
+            scales[i] = front.tile([P, PASSES * P], U8, tag="scales", name="h_scales", align_bytes=64)
+            nc.vector.quantize_mx(out=codes[i][:].bitcast(FP8X4), scales=scales[i][:], in_=grouped[i][:])
+
+        def multiply(i):
+            acc[i] = psum.tile([P, CHANNELS], F32, tag="acc", name="acc")
+            for g in range(PASSES):
+                nc.tensor.matmul_mx(
+                    out=acc[i][:],
+                    lhsT=codes[i][:, g * P : (g + 1) * P].bitcast(FP8X4),
+                    lhsT_scale=scales[i][:, g * P : (g + 1) * P],
+                    rhs=w_codes[:, g, :].bitcast(FP8X4),
+                    rhs_scale=w_scales[:, g, :],
+                    start=(g == 0),
+                    stop=(g == PASSES - 1),
+                )
+
+        def moments_of(i):
+            v[i] = back.tile([P, CHANNELS], F32, tag="v", name="v")
+            nc.vector.tensor_tensor(
+                out=v[i][:], in0=acc[i][:], in1=bias_all[:].rearrange("p t r -> p (t r)"), op=ALU.add
+            )
+            stats = small.tile([P, 6], F32, tag="stats")
+            nc.vector.bn_stats(out=stats[:], in_=v[i][:])
+            moments[i] = small.tile([P, 2], F32, tag="moments", name="moments")
+            nc.vector.bn_aggr(out=moments[i][:], in_=stats[:])
+            var_u = small.tile([P, 1], F32, tag="var_u")
+            nc.vector.tensor_scalar(
+                out=var_u[:], in0=moments[i][:, 1:2], scalar1=s_ffn_sq[:], scalar2=EPS, op0=ALU.mult, op1=ALU.add
+            )
+            std[i] = small.tile([P, 1], F32, tag="std", name="std")
+            nc.scalar.sqrt(out=std[i][:], in_=var_u[:])
+
+        def normalise(i):
+            inv_std = small.tile([P, 1], F32, tag="inv_std")
+            nc.vector.reciprocal(out=inv_std[:], in_=std[i][:])
+            offset = small.tile([P, 1], F32, tag="offset")
+            nc.vector.scalar_tensor_tensor(
+                out=offset[:], in0=moments[i][:, 0:1], scalar=-1.0, in1=inv_std[:], op0=ALU.mult, op1=ALU.mult
+            )
+            normed[i] = back.tile([P, CHANNELS], F32, tag="normed", name="normed")
+            nc.scalar.activation(
+                out=normed[i][:], in_=v[i][:], func=ACT.Identity, bias=offset[:], scale=inv_std[:]
+            )
+
+        def transpose_out(i):
+            b = i // TILES_IMAGE
+            part = i % TILES_IMAGE
+            if part == 0:
+                turned[b] = [
+                    psum.tile([P, 2, IMAGE_PIXELS], F32, tag="turned", name="turned%d" % half) for half in range(2)
+                ]
+            for t in range(CH_BLOCKS):
+                nc.tensor.transpose(
+                    turned[b][t // 2][:, t % 2, part * P : (part + 1) * P],
+                    normed[i][:, t * P : (t + 1) * P],
+                    ident[:],
+                )
+
+        def finish(b):
+            summed = image.tile([P, CH_BLOCKS, IMAGE_PIXELS], F32, tag="summed")
+            result = image.tile([P, CH_BLOCKS, IMAGE_PIXELS], F32, tag="result")
+            for t in range(CH_BLOCKS):
+                nc.vector.scalar_tensor_tensor(
+                    out=summed[:, t, :],
+                    in0=turned[b][t // 2][:, t % 2, :],
+                    scalar=gain[:, t : t + 1],
+                    in1=x_raw[b][:, t * IMAGE_PIXELS : (t + 1) * IMAGE_PIXELS],
+                    op0=ALU.mult,
+                    op1=ALU.add,
+                )
+            for t in range(CH_BLOCKS):
+                nc.scalar.activation(
+                    out=result[:, t, :], in_=summed[:, t, :], func=ACT.Relu, bias=shift[:, t : t + 1], scale=1.0
+                )
+                if t % 2 == 1:
+                    nc.sync.dma_start(
+                        out=out_images[:, b, (t - 1) * IMAGE_PIXELS : (t + 1) * IMAGE_PIXELS],
+                        in_=result[:, t - 1 : t + 1, :].rearrange("p t c -> p (t c)"),
+                    )
+
+        for i in range(-2, TILES + 2):
+            if 0 <= i + 2 < TILES:
+                transpose_h(i + 2)
+            if 0 <= i - 2 < TILES:
+                transpose_out(i - 2)
+            if 0 <= i < TILES:
+                multiply(i)
+            if 0 <= i - 1 < TILES:
+                moments_of(i - 1)
+            if 0 <= i + 1 < TILES:
+                quantise_h(i + 1)
+            if 0 <= i - 1 < TILES:
+                normalise(i - 1)
+            if 0 <= i - 2 < TILES and (i - 2) % TILES_IMAGE == TILES_IMAGE - 1:
+                finish((i - 2) // TILES_IMAGE)
+
+
+def load_x(nc, pool, x_images, x_raw):
+    b = len(x_raw)
+    x_tile = pool.tile([P, CH_BLOCKS * IMAGE_PIXELS], BF16, name="x_raw%d" % b)
+    nc.sync.dma_start(out=x_tile[:], in_=x_images[:, b, :])
+    x_raw.append(x_tile)
+
+
+def k_to_partitions(nc, psum, rows, ident, grouped, copiers):
+    words = rows[:].bitcast(F32)
+    grouped_words = grouped[:].bitcast(F32).rearrange("p (g r u) -> p g r u", g=PASSES, u=2)
+    for half in range(2):
+        bank = psum.tile([P, 2, 2, P], F32, tag="bank", bufs=4)
+        for g in range(2):
+            for u in range(2):
+                first = (2 * half + g) * WORDS_PASS + u * P
+                nc.tensor.transpose(bank[:, g, u, :], words[:, first : first + P], ident[:])
+        copiers[half](
+            out=grouped_words[:, 2 * half : 2 * half + 2, :, :], in_=bank[:].rearrange("p g u r -> p g r u")
+        )

@@ -24,6 +24,9 @@ TILES = IMAGES * IMAGE_PIXELS // P
 TILES_IMAGE = IMAGE_PIXELS // P
 EPS = 1e-5
 
+AHEAD = 2
+BEHIND = 4
+
 FLOPS = 2 * IMAGES * IMAGE_PIXELS * CHANNELS * K
 
 
@@ -43,7 +46,6 @@ def tile_transformerconvblock_pc_kernel(
         raw = stack.enter_context(tc.tile_pool(name="raw", bufs=1))
         front = stack.enter_context(tc.tile_pool(name="front", bufs=3))
         back = stack.enter_context(tc.tile_pool(name="back", bufs=3))
-        small = stack.enter_context(tc.tile_pool(name="small", bufs=4))
         image = stack.enter_context(tc.tile_pool(name="image", bufs=2))
         psum = stack.enter_context(tc.psum_pool(name="psum", bufs=2))
 
@@ -65,7 +67,7 @@ def tile_transformerconvblock_pc_kernel(
         nc.scalar.dma_start(out=shift_raw[:], in_=ln2_b.rearrange("(r t) -> r t", t=CH_BLOCKS))
 
         warm = const.tile([P, 1], F32)
-        nc.scalar.sqrt(out=warm[:], in_=ones[:, 0:1])
+        nc.scalar.activation(out=warm[:], in_=ones[:, 0:1], func=ACT.Abs_reciprocal_sqrt)
 
         w_raw = []
         for t in range(CH_BLOCKS):
@@ -85,6 +87,29 @@ def tile_transformerconvblock_pc_kernel(
         ident = const.tile([P, P], F32)
         make_identity(nc, ident[:])
 
+        bias_ps = psum.tile([P, CHANNELS], F32, tag="acc")
+        nc.tensor.matmul(out=bias_ps[:], lhsT=ones[:], rhs=vec_rows[:, 0:CHANNELS], start=True, stop=True)
+        mult_ps = psum.tile([P, 32], F32, tag="acc")
+        nc.tensor.matmul(
+            out=mult_ps[:], lhsT=ones[:], rhs=vec_rows[:, CHANNELS : CHANNELS + 32], start=True, stop=True
+        )
+        bias_all = const.tile([P, CH_BLOCKS, P], F32)
+        nc.vector.tensor_copy(out=bias_all[:], in_=bias_ps[:].rearrange("p (r t) -> p t r", t=CH_BLOCKS))
+        mult = const.tile([P, 32], F32)
+        nc.vector.tensor_copy(out=mult[:], in_=mult_ps[:])
+        s_ffn = mult[:, 0:1]
+        s_norm = mult[:, 16:17]
+        eps = const.tile([P, 1], F32)
+        nc.vector.tensor_scalar_mul(out=eps[:], in0=ones[:, 0:1], scalar1=EPS)
+        shift = const.tile([P, CH_BLOCKS], F32)
+        nc.vector.tensor_scalar_mul(out=shift[:], in0=shift_raw[:], scalar1=s_norm)
+        gain = const.tile([P, CH_BLOCKS], F32)
+        nc.vector.tensor_scalar(
+            out=gain[:], in0=gain_raw[:], scalar1=s_norm, scalar2=s_ffn, op0=ALU.mult, op1=ALU.mult
+        )
+        s_ffn_sq = const.tile([P, 1], F32)
+        nc.vector.tensor_mul(out=s_ffn_sq[:], in0=s_ffn, in1=s_ffn)
+
         w_codes = const.tile([P, PASSES, CHANNELS], U32, align_bytes=64)
         w_scales = const.tile([P, PASSES, CHANNELS], U8, align_bytes=64)
         for t in range(CH_BLOCKS):
@@ -97,32 +122,12 @@ def tile_transformerconvblock_pc_kernel(
                     in_=w_grouped[:, g * P * 4 : (g + 1) * P * 4],
                 )
 
-        bias_ps = psum.tile([P, CHANNELS], F32, tag="acc")
-        nc.tensor.matmul(out=bias_ps[:], lhsT=ones[:], rhs=vec_rows[:, 0:CHANNELS], start=True, stop=True)
-        mult_ps = psum.tile([P, 32], F32, tag="acc")
-        nc.tensor.matmul(out=mult_ps[:], lhsT=ones[:], rhs=vec_rows[:, CHANNELS : CHANNELS + 32], start=True, stop=True)
-        bias_all = const.tile([P, CH_BLOCKS, P], F32)
-        nc.vector.tensor_copy(out=bias_all[:], in_=bias_ps[:].rearrange("p (r t) -> p t r", t=CH_BLOCKS))
-        mult = const.tile([P, 32], F32)
-        nc.vector.tensor_copy(out=mult[:], in_=mult_ps[:])
-        s_ffn = mult[:, 0:1]
-        s_norm = mult[:, 16:17]
-        s_ffn_sq = const.tile([P, 1], F32)
-        nc.vector.tensor_mul(out=s_ffn_sq[:], in0=s_ffn, in1=s_ffn)
-        gain = const.tile([P, CH_BLOCKS], F32)
-        nc.vector.tensor_scalar(
-            out=gain[:], in0=gain_raw[:], scalar1=s_norm, scalar2=s_ffn, op0=ALU.mult, op1=ALU.mult
-        )
-        shift = const.tile([P, CH_BLOCKS], F32)
-        nc.vector.tensor_scalar_mul(out=shift[:], in0=shift_raw[:], scalar1=s_norm)
-
         grouped = {}
         codes = {}
         scales = {}
         acc = {}
         v = {}
-        moments = {}
-        std = {}
+        stats = {}
         normed = {}
         turned = {}
 
@@ -148,47 +153,43 @@ def tile_transformerconvblock_pc_kernel(
                     stop=(g == PASSES - 1),
                 )
 
-        def moments_of(i):
+        def add_bias(i):
             v[i] = back.tile([P, CHANNELS], F32, tag="v", name="v")
             nc.vector.tensor_tensor(
                 out=v[i][:], in0=acc[i][:], in1=bias_all[:].rearrange("p t r -> p (t r)"), op=ALU.add
             )
-            stats = small.tile([P, 6], F32, tag="stats")
-            nc.vector.bn_stats(out=stats[:], in_=v[i][:])
-            moments[i] = small.tile([P, 2], F32, tag="moments", name="moments")
-            nc.vector.bn_aggr(out=moments[i][:], in_=stats[:])
-            var_u = small.tile([P, 1], F32, tag="var_u")
-            nc.vector.tensor_scalar(
-                out=var_u[:], in0=moments[i][:, 1:2], scalar1=s_ffn_sq[:], scalar2=EPS, op0=ALU.mult, op1=ALU.add
-            )
-            std[i] = small.tile([P, 1], F32, tag="std", name="std")
-            nc.scalar.sqrt(out=std[i][:], in_=var_u[:])
+
+        def sum_up(i):
+            stats[i] = back.tile([P, 6], F32, tag="stats", name="stats")
+            nc.vector.bn_stats(out=stats[i][:], in_=v[i][:])
 
         def normalise(i):
-            inv_std = small.tile([P, 1], F32, tag="inv_std")
-            nc.vector.reciprocal(out=inv_std[:], in_=std[i][:])
-            offset = small.tile([P, 1], F32, tag="offset")
-            nc.vector.scalar_tensor_tensor(
-                out=offset[:], in0=moments[i][:, 0:1], scalar=-1.0, in1=inv_std[:], op0=ALU.mult, op1=ALU.mult
+            moments = back.tile([P, 2], F32, tag="moments")
+            nc.vector.bn_aggr(out=moments[:], in_=stats[i][:])
+            neg_mean = back.tile([P, 1], F32, tag="neg_mean")
+            nc.gpsimd.tensor_scalar(
+                out=neg_mean[:], in0=moments[:, 0:1], scalar1=-1.0, scalar2=0.0, op0=ALU.mult, op1=ALU.add
             )
-            normed[i] = back.tile([P, CHANNELS], F32, tag="normed", name="normed")
+            inv_std = back.tile([P, 1], F32, tag="inv_std")
             nc.scalar.activation(
-                out=normed[i][:], in_=v[i][:], func=ACT.Identity, bias=offset[:], scale=inv_std[:]
+                out=inv_std[:], in_=moments[:, 1:2], func=ACT.Abs_reciprocal_sqrt, bias=eps[:], scale=s_ffn_sq[:]
+            )
+            normed[i] = back.tile([P, CHANNELS], F32, tag="normed", name="normed", bufs=5)
+            nc.gpsimd.tensor_scalar(
+                out=normed[i][:], in0=v[i][:], scalar1=neg_mean[:], scalar2=inv_std[:], op0=ALU.add, op1=ALU.mult
             )
 
-        def transpose_out(i):
-            b = i // TILES_IMAGE
-            part = i % TILES_IMAGE
-            if part == 0:
-                turned[b] = [
-                    psum.tile([P, 2, IMAGE_PIXELS], F32, tag="turned", name="turned%d" % half) for half in range(2)
-                ]
-            for t in range(CH_BLOCKS):
-                nc.tensor.transpose(
-                    turned[b][t // 2][:, t % 2, part * P : (part + 1) * P],
-                    normed[i][:, t * P : (t + 1) * P],
-                    ident[:],
-                )
+        def turn_back(b):
+            turned[b] = [
+                psum.tile([P, 2, IMAGE_PIXELS], F32, tag="turned", name="turned%d" % half) for half in range(2)
+            ]
+            for part in range(TILES_IMAGE):
+                for t in range(CH_BLOCKS):
+                    nc.tensor.transpose(
+                        turned[b][t // 2][:, t % 2, part * P : (part + 1) * P],
+                        normed[b * TILES_IMAGE + part][:, t * P : (t + 1) * P],
+                        ident[:],
+                    )
 
         def finish(b):
             summed = image.tile([P, CH_BLOCKS, IMAGE_PIXELS], F32, tag="summed")
@@ -212,21 +213,23 @@ def tile_transformerconvblock_pc_kernel(
                         in_=result[:, t - 1 : t + 1, :].rearrange("p t c -> p (t c)"),
                     )
 
-        for i in range(-2, TILES + 2):
-            if 0 <= i + 2 < TILES:
-                transpose_h(i + 2)
-            if 0 <= i - 2 < TILES:
-                transpose_out(i - 2)
+        for i in range(-AHEAD, TILES + BEHIND):
+            image_done = (i - BEHIND) // TILES_IMAGE if (i - BEHIND) % TILES_IMAGE == 0 else -1
+            if 0 <= i + AHEAD < TILES:
+                transpose_h(i + AHEAD)
+            if 0 <= image_done < IMAGES:
+                turn_back(image_done)
             if 0 <= i < TILES:
                 multiply(i)
-            if 0 <= i - 1 < TILES:
-                moments_of(i - 1)
-            if 0 <= i + 1 < TILES:
-                quantise_h(i + 1)
+                add_bias(i)
             if 0 <= i - 1 < TILES:
                 normalise(i - 1)
-            if 0 <= i - 2 < TILES and (i - 2) % TILES_IMAGE == TILES_IMAGE - 1:
-                finish((i - 2) // TILES_IMAGE)
+            if 0 <= image_done < IMAGES:
+                finish(image_done)
+            if 0 <= i + AHEAD < TILES:
+                quantise_h(i + AHEAD)
+            if 0 <= i < TILES:
+                sum_up(i)
 
 
 def load_x(nc, pool, x_images, x_raw):

@@ -69,46 +69,17 @@ def tile_transformerconvblock_pc_kernel(
         warm = const.tile([P, 1], F32)
         nc.scalar.activation(out=warm[:], in_=ones[:, 0:1], func=ACT.Abs_reciprocal_sqrt)
 
-        w_raw = []
-        for t in range(CH_BLOCKS):
-            w_tile = raw.tile([P, K], BF16, name="w_raw%d" % t)
-            nc.sync.dma_start(out=w_tile[:], in_=w_blocks[:, t, :])
-            w_raw.append(w_tile)
+        w_raw = [load_rows(nc, raw, w_blocks[:, t, :], "w_raw%d" % t, 1) for t in range(CH_BLOCKS)]
         h_raw = []
         x_raw = []
         for i in range(TILES):
-            h_tile = raw.tile([P, K], BF16, name="h_raw%d" % i)
-            nc.sync.dma_start(out=h_tile[:], in_=h_rows[i * P : (i + 1) * P, :])
-            h_raw.append(h_tile)
+            h_raw.append(load_rows(nc, raw, h_rows[i * P : (i + 1) * P, :], "h_raw%d" % i, 2))
             if i >= TILES_IMAGE and i % TILES_IMAGE == 1:
                 load_x(nc, raw, x_images, x_raw)
         load_x(nc, raw, x_images, x_raw)
 
         ident = const.tile([P, P], F32)
         make_identity(nc, ident[:])
-
-        bias_ps = psum.tile([P, CHANNELS], F32, tag="acc")
-        nc.tensor.matmul(out=bias_ps[:], lhsT=ones[:], rhs=vec_rows[:, 0:CHANNELS], start=True, stop=True)
-        mult_ps = psum.tile([P, 32], F32, tag="acc")
-        nc.tensor.matmul(
-            out=mult_ps[:], lhsT=ones[:], rhs=vec_rows[:, CHANNELS : CHANNELS + 32], start=True, stop=True
-        )
-        bias_all = const.tile([P, CH_BLOCKS, P], F32)
-        nc.vector.tensor_copy(out=bias_all[:], in_=bias_ps[:].rearrange("p (r t) -> p t r", t=CH_BLOCKS))
-        mult = const.tile([P, 32], F32)
-        nc.vector.tensor_copy(out=mult[:], in_=mult_ps[:])
-        s_ffn = mult[:, 0:1]
-        s_norm = mult[:, 16:17]
-        eps = const.tile([P, 1], F32)
-        nc.vector.tensor_scalar_mul(out=eps[:], in0=ones[:, 0:1], scalar1=EPS)
-        shift = const.tile([P, CH_BLOCKS], F32)
-        nc.vector.tensor_scalar_mul(out=shift[:], in0=shift_raw[:], scalar1=s_norm)
-        gain = const.tile([P, CH_BLOCKS], F32)
-        nc.vector.tensor_scalar(
-            out=gain[:], in0=gain_raw[:], scalar1=s_norm, scalar2=s_ffn, op0=ALU.mult, op1=ALU.mult
-        )
-        s_ffn_sq = const.tile([P, 1], F32)
-        nc.vector.tensor_mul(out=s_ffn_sq[:], in0=s_ffn, in1=s_ffn)
 
         w_codes = const.tile([P, PASSES, CHANNELS], U32, align_bytes=64)
         w_scales = const.tile([P, PASSES, CHANNELS], U8, align_bytes=64)
@@ -121,6 +92,31 @@ def tile_transformerconvblock_pc_kernel(
                     scales=w_scales[:, g, t * P : (t + 1) * P],
                     in_=w_grouped[:, g * P * 4 : (g + 1) * P * 4],
                 )
+
+        bias_all = const.tile([P, CH_BLOCKS, P], F32)
+        mult = const.tile([P, 32], F32)
+        s_ffn = mult[:, 0:1]
+        s_norm = mult[:, 16:17]
+        s_ffn_sq = const.tile([P, 1], F32)
+        eps = const.tile([P, 1], F32)
+        gain = const.tile([P, CH_BLOCKS], F32)
+        shift = const.tile([P, CH_BLOCKS], F32)
+
+        def spread_constants():
+            bias_ps = psum.tile([P, CHANNELS], F32, tag="turned")
+            nc.tensor.matmul(out=bias_ps[:], lhsT=ones[:], rhs=vec_rows[:, 0:CHANNELS], start=True, stop=True)
+            mult_ps = psum.tile([P, 32], F32, tag="turned")
+            nc.tensor.matmul(
+                out=mult_ps[:], lhsT=ones[:], rhs=vec_rows[:, CHANNELS : CHANNELS + 32], start=True, stop=True
+            )
+            nc.vector.tensor_copy(out=bias_all[:], in_=bias_ps[:].rearrange("p (r t) -> p t r", t=CH_BLOCKS))
+            nc.vector.tensor_copy(out=mult[:], in_=mult_ps[:])
+            nc.vector.tensor_scalar_mul(out=eps[:], in0=ones[:, 0:1], scalar1=EPS)
+            nc.vector.tensor_scalar_mul(out=shift[:], in0=shift_raw[:], scalar1=s_norm)
+            nc.vector.tensor_scalar(
+                out=gain[:], in0=gain_raw[:], scalar1=s_norm, scalar2=s_ffn, op0=ALU.mult, op1=ALU.mult
+            )
+            nc.vector.tensor_mul(out=s_ffn_sq[:], in0=s_ffn, in1=s_ffn)
 
         grouped = {}
         codes = {}
@@ -138,7 +134,12 @@ def tile_transformerconvblock_pc_kernel(
         def quantise_h(i):
             codes[i] = front.tile([P, PASSES * P], U32, tag="codes", name="h_codes", align_bytes=64)
             scales[i] = front.tile([P, PASSES * P], U8, tag="scales", name="h_scales", align_bytes=64)
-            nc.vector.quantize_mx(out=codes[i][:].bitcast(FP8X4), scales=scales[i][:], in_=grouped[i][:])
+            for half in range(2):
+                nc.vector.quantize_mx(
+                    out=codes[i][:, half * 2 * P : (half + 1) * 2 * P].bitcast(FP8X4),
+                    scales=scales[i][:, half * 2 * P : (half + 1) * 2 * P],
+                    in_=grouped[i][:, half * 8 * P : (half + 1) * 8 * P],
+                )
 
         def multiply(i):
             acc[i] = psum.tile([P, CHANNELS], F32, tag="acc", name="acc")
@@ -207,29 +208,45 @@ def tile_transformerconvblock_pc_kernel(
                 nc.scalar.activation(
                     out=result[:, t, :], in_=summed[:, t, :], func=ACT.Relu, bias=shift[:, t : t + 1], scale=1.0
                 )
-                if t % 2 == 1:
-                    nc.sync.dma_start(
-                        out=out_images[:, b, (t - 1) * IMAGE_PIXELS : (t + 1) * IMAGE_PIXELS],
-                        in_=result[:, t - 1 : t + 1, :].rearrange("p t c -> p (t c)"),
-                    )
+                nc.sync.dma_start(
+                    out=out_images[:, b, t * IMAGE_PIXELS : (t + 1) * IMAGE_PIXELS], in_=result[:, t, :]
+                )
 
-        for i in range(-AHEAD, TILES + BEHIND):
+        transpose_h(0)
+        quantise_h(0)
+        spread_constants()
+        for i in range(1, AHEAD):
+            transpose_h(i)
+            quantise_h(i)
+        for i in range(TILES + BEHIND):
             image_done = (i - BEHIND) // TILES_IMAGE if (i - BEHIND) % TILES_IMAGE == 0 else -1
-            if 0 <= i + AHEAD < TILES:
+            if i < TILES:
+                multiply(i)
+            if i + AHEAD < TILES:
                 transpose_h(i + AHEAD)
             if 0 <= image_done < IMAGES:
                 turn_back(image_done)
-            if 0 <= i < TILES:
-                multiply(i)
+            if i < TILES:
                 add_bias(i)
             if 0 <= i - 1 < TILES:
                 normalise(i - 1)
             if 0 <= image_done < IMAGES:
                 finish(image_done)
-            if 0 <= i + AHEAD < TILES:
+            if i + AHEAD < TILES:
                 quantise_h(i + AHEAD)
-            if 0 <= i < TILES:
+            if i < TILES:
                 sum_up(i)
+
+
+def load_rows(nc, pool, rows, name, pieces):
+    width = K // pieces
+    halves = []
+    for piece in range(pieces):
+        part = pool.tile([P, width], BF16, name="%s_%d" % (name, piece))
+        nc.sync.dma_start(out=part[:], in_=rows[:, piece * width : (piece + 1) * width])
+        for j in range(2 // pieces):
+            halves.append(part[:, j * (K // 2) : (j + 1) * (K // 2)])
+    return halves
 
 
 def load_x(nc, pool, x_images, x_raw):
@@ -240,13 +257,13 @@ def load_x(nc, pool, x_images, x_raw):
 
 
 def k_to_partitions(nc, psum, rows, ident, grouped, copiers):
-    words = rows[:].bitcast(F32)
     grouped_words = grouped[:].bitcast(F32).rearrange("p (g r u) -> p g r u", g=PASSES, u=2)
     for half in range(2):
+        words = rows[half].bitcast(F32)
         bank = psum.tile([P, 2, 2, P], F32, tag="bank", bufs=4)
         for g in range(2):
             for u in range(2):
-                first = (2 * half + g) * WORDS_PASS + u * P
+                first = g * WORDS_PASS + u * P
                 nc.tensor.transpose(bank[:, g, u, :], words[:, first : first + P], ident[:])
         copiers[half](
             out=grouped_words[:, 2 * half : 2 * half + 2, :, :], in_=bank[:].rearrange("p g u r -> p g r u")

@@ -25,7 +25,8 @@ TILES_IMAGE = IMAGE_PIXELS // P
 EPS = 1e-5
 
 AHEAD = 2
-BEHIND = 4
+BEHIND = 6
+TURN_BANKS = 6
 
 FLOPS = 2 * IMAGES * IMAGE_PIXELS * CHANNELS * K
 
@@ -46,7 +47,7 @@ def tile_transformerconvblock_pc_kernel(
         raw = stack.enter_context(tc.tile_pool(name="raw", bufs=1))
         front = stack.enter_context(tc.tile_pool(name="front", bufs=3))
         back = stack.enter_context(tc.tile_pool(name="back", bufs=3))
-        image = stack.enter_context(tc.tile_pool(name="image", bufs=2))
+        image = stack.enter_context(tc.tile_pool(name="image", bufs=3))
         psum = stack.enter_context(tc.psum_pool(name="psum", bufs=2))
 
         vec_rows = const.tile([P, CHANNELS + 32], BF16)
@@ -103,9 +104,9 @@ def tile_transformerconvblock_pc_kernel(
         shift = const.tile([P, CH_BLOCKS], F32)
 
         def spread_constants():
-            bias_ps = psum.tile([P, CHANNELS], F32, tag="turned")
+            bias_ps = psum.tile([P, CHANNELS], F32, tag="bank", bufs=TURN_BANKS)
             nc.tensor.matmul(out=bias_ps[:], lhsT=ones[:], rhs=vec_rows[:, 0:CHANNELS], start=True, stop=True)
-            mult_ps = psum.tile([P, 32], F32, tag="turned")
+            mult_ps = psum.tile([P, 32], F32, tag="bank", bufs=TURN_BANKS)
             nc.tensor.matmul(
                 out=mult_ps[:], lhsT=ones[:], rhs=vec_rows[:, CHANNELS : CHANNELS + 32], start=True, stop=True
             )
@@ -175,14 +176,15 @@ def tile_transformerconvblock_pc_kernel(
             nc.scalar.activation(
                 out=inv_std[:], in_=moments[:, 1:2], func=ACT.Abs_reciprocal_sqrt, bias=eps[:], scale=s_ffn_sq[:]
             )
-            normed[i] = back.tile([P, CHANNELS], F32, tag="normed", name="normed", bufs=5)
+            normed[i] = back.tile([P, CHANNELS], F32, tag="normed", name="normed", bufs=BEHIND + 1)
             nc.gpsimd.tensor_scalar(
                 out=normed[i][:], in0=v[i][:], scalar1=neg_mean[:], scalar2=inv_std[:], op0=ALU.add, op1=ALU.mult
             )
 
         def turn_back(b):
             turned[b] = [
-                psum.tile([P, 2, IMAGE_PIXELS], F32, tag="turned", name="turned%d" % half) for half in range(2)
+                psum.tile([P, 2, IMAGE_PIXELS], F32, tag="bank", name="turned%d" % half, bufs=TURN_BANKS)
+                for half in range(2)
             ]
             for part in range(TILES_IMAGE):
                 for t in range(CH_BLOCKS):
@@ -260,7 +262,7 @@ def k_to_partitions(nc, psum, rows, ident, grouped, copiers):
     grouped_words = grouped[:].bitcast(F32).rearrange("p (g r u) -> p g r u", g=PASSES, u=2)
     for half in range(2):
         words = rows[half].bitcast(F32)
-        bank = psum.tile([P, 2, 2, P], F32, tag="bank", bufs=4)
+        bank = psum.tile([P, 2, 2, P], F32, tag="bank", bufs=TURN_BANKS)
         for g in range(2):
             for u in range(2):
                 first = g * WORDS_PASS + u * P

@@ -12,20 +12,29 @@ ALU = mybir.AluOpType
 ACT = mybir.ActivationFunctionType
 
 P = 128
+PACK = 4
 K = 2048
-K_PASS = 512
+K_PASS = P * PACK
 PASSES = K // K_PASS
-WORDS_PASS = K_PASS // 2
+K_HALF = K // 2
+PAIRS_PASS = K_PASS // 2
 CHANNELS = 512
 CH_BLOCKS = CHANNELS // P
 IMAGES = 4
 IMAGE_PIXELS = 256
-TILES = IMAGES * IMAGE_PIXELS // P
 TILES_IMAGE = IMAGE_PIXELS // P
+TILES = IMAGES * TILES_IMAGE
 EPS = 1e-5
+
+MULT_COLS = 32
+S_FFN_COL = 0
+S_NORM_COL = 16
 
 AHEAD = 2
 BEHIND = 6
+STEPS = (TILES - TILES_IMAGE) + BEHIND + 1
+assert STEPS > TILES
+PRODUCT_BANKS = 2
 TURN_BANKS = 6
 
 FLOPS = 2 * IMAGES * IMAGE_PIXELS * CHANNELS * K
@@ -39,45 +48,39 @@ def tile_transformerconvblock_pc_kernel(
     h_rows = h.rearrange("b i j k -> (b i j) k")
     w_blocks = ffn2_w.rearrange("(r t) k -> r t k", t=CH_BLOCKS)
     x_images = x.rearrange("b (r t) i j -> r b (t i j)", t=CH_BLOCKS)
-    out_images = out.rearrange("b (r t) i j -> r b (t i j)", t=CH_BLOCKS)
+    out_blocks = out.rearrange("b (r t) i j -> r b t (i j)", t=CH_BLOCKS)
 
     with ExitStack() as stack:
         stack.enter_context(tc.manual_schedule())
         const = stack.enter_context(tc.tile_pool(name="const", bufs=1))
         raw = stack.enter_context(tc.tile_pool(name="raw", bufs=1))
-        front = stack.enter_context(tc.tile_pool(name="front", bufs=3))
+        front = stack.enter_context(tc.tile_pool(name="front", bufs=AHEAD + 1))
         back = stack.enter_context(tc.tile_pool(name="back", bufs=3))
         image = stack.enter_context(tc.tile_pool(name="image", bufs=3))
-        psum = stack.enter_context(tc.psum_pool(name="psum", bufs=2))
+        psum = stack.enter_context(tc.psum_pool(name="psum", bufs=PRODUCT_BANKS))
 
-        vec_rows = const.tile([P, CHANNELS + 32], BF16)
+        vec_rows = const.tile([P, CHANNELS + MULT_COLS], BF16)
         nc.vector.memset(vec_rows[:], 0.0)
         ones = const.tile([P, P], BF16)
         nc.vector.memset(ones[:], 1.0)
         nc.scalar.dma_start(out=vec_rows[0:1, 0:CHANNELS], in_=ffn2_b.rearrange("(o c) -> o c", o=1))
-        nc.scalar.dma_start(
-            out=vec_rows[0:1, CHANNELS : CHANNELS + 1], in_=scale_ffn.rearrange("(o c) -> o c", o=1)
-        )
-        nc.scalar.dma_start(
-            out=vec_rows[0:1, CHANNELS + 16 : CHANNELS + 17],
-            in_=scale_norm2.rearrange("(o c) -> o c", o=1),
-        )
-        gain_raw = const.tile([P, CH_BLOCKS], BF16)
-        nc.scalar.dma_start(out=gain_raw[:], in_=ln2_w.rearrange("(r t) -> r t", t=CH_BLOCKS))
-        shift_raw = const.tile([P, CH_BLOCKS], BF16)
-        nc.scalar.dma_start(out=shift_raw[:], in_=ln2_b.rearrange("(r t) -> r t", t=CH_BLOCKS))
+        for column, multiplier in ((S_FFN_COL, scale_ffn), (S_NORM_COL, scale_norm2)):
+            nc.scalar.dma_start(
+                out=vec_rows[0:1, CHANNELS + column : CHANNELS + column + 1],
+                in_=multiplier.rearrange("(o c) -> o c", o=1),
+            )
+        ln2_w_raw = const.tile([P, CH_BLOCKS], BF16)
+        nc.scalar.dma_start(out=ln2_w_raw[:], in_=ln2_w.rearrange("(r t) -> r t", t=CH_BLOCKS))
+        ln2_b_raw = const.tile([P, CH_BLOCKS], BF16)
+        nc.scalar.dma_start(out=ln2_b_raw[:], in_=ln2_b.rearrange("(r t) -> r t", t=CH_BLOCKS))
 
-        warm = const.tile([P, 1], F32)
-        nc.scalar.activation(out=warm[:], in_=ones[:, 0:1], func=ACT.Abs_reciprocal_sqrt)
+        table_warmer = const.tile([P, 1], F32)
+        nc.scalar.activation(out=table_warmer[:], in_=ones[:, 0:1], func=ACT.Abs_reciprocal_sqrt)
 
         w_raw = [load_rows(nc, raw, w_blocks[:, t, :], "w_raw%d" % t, 1) for t in range(CH_BLOCKS)]
-        h_raw = []
-        x_raw = []
-        for i in range(TILES):
-            h_raw.append(load_rows(nc, raw, h_rows[i * P : (i + 1) * P, :], "h_raw%d" % i, 2))
-            if i >= TILES_IMAGE and i % TILES_IMAGE == 1:
-                load_x(nc, raw, x_images, x_raw)
-        load_x(nc, raw, x_images, x_raw)
+        h_raw = [load_rows(nc, raw, h_rows[i * P : (i + 1) * P, :], "h_raw%d" % i, 2) for i in range(TILES)]
+        x_raw = raw.tile([P, IMAGES, CH_BLOCKS, IMAGE_PIXELS], BF16)
+        nc.sync.dma_start(out=x_raw[:].rearrange("p b t c -> p b (t c)"), in_=x_images)
 
         ident = const.tile([P, P], F32)
         make_identity(nc, ident[:])
@@ -85,19 +88,19 @@ def tile_transformerconvblock_pc_kernel(
         w_codes = const.tile([P, PASSES, CHANNELS], U32, align_bytes=64)
         w_scales = const.tile([P, PASSES, CHANNELS], U8, align_bytes=64)
         for t in range(CH_BLOCKS):
-            w_grouped = front.tile([P, PASSES * P * 4], BF16, tag="grouped", align_bytes=64)
+            w_grouped = front.tile([P, PASSES * P * PACK], BF16, tag="grouped", align_bytes=64)
             k_to_partitions(nc, psum, w_raw[t], ident, w_grouped, (nc.scalar.copy, nc.vector.tensor_copy))
             for g in range(PASSES):
                 nc.vector.quantize_mx(
                     out=w_codes[:, g, t * P : (t + 1) * P].bitcast(FP8X4),
                     scales=w_scales[:, g, t * P : (t + 1) * P],
-                    in_=w_grouped[:, g * P * 4 : (g + 1) * P * 4],
+                    in_=w_grouped[:, g * P * PACK : (g + 1) * P * PACK],
                 )
 
         bias_all = const.tile([P, CH_BLOCKS, P], F32)
-        mult = const.tile([P, 32], F32)
-        s_ffn = mult[:, 0:1]
-        s_norm = mult[:, 16:17]
+        mult = const.tile([P, MULT_COLS], F32)
+        s_ffn = mult[:, S_FFN_COL : S_FFN_COL + 1]
+        s_norm = mult[:, S_NORM_COL : S_NORM_COL + 1]
         s_ffn_sq = const.tile([P, 1], F32)
         eps = const.tile([P, 1], F32)
         gain = const.tile([P, CH_BLOCKS], F32)
@@ -106,47 +109,45 @@ def tile_transformerconvblock_pc_kernel(
         def spread_constants():
             bias_ps = psum.tile([P, CHANNELS], F32, tag="bank", bufs=TURN_BANKS)
             nc.tensor.matmul(out=bias_ps[:], lhsT=ones[:], rhs=vec_rows[:, 0:CHANNELS], start=True, stop=True)
-            mult_ps = psum.tile([P, 32], F32, tag="bank", bufs=TURN_BANKS)
-            nc.tensor.matmul(
-                out=mult_ps[:], lhsT=ones[:], rhs=vec_rows[:, CHANNELS : CHANNELS + 32], start=True, stop=True
-            )
+            mult_ps = psum.tile([P, MULT_COLS], F32, tag="bank", bufs=TURN_BANKS)
+            nc.tensor.matmul(out=mult_ps[:], lhsT=ones[:], rhs=vec_rows[:, CHANNELS:], start=True, stop=True)
             nc.vector.tensor_copy(out=bias_all[:], in_=bias_ps[:].rearrange("p (r t) -> p t r", t=CH_BLOCKS))
             nc.vector.tensor_copy(out=mult[:], in_=mult_ps[:])
             nc.vector.tensor_scalar_mul(out=eps[:], in0=ones[:, 0:1], scalar1=EPS)
-            nc.vector.tensor_scalar_mul(out=shift[:], in0=shift_raw[:], scalar1=s_norm)
+            nc.vector.tensor_scalar_mul(out=shift[:], in0=ln2_b_raw[:], scalar1=s_norm)
             nc.vector.tensor_scalar(
-                out=gain[:], in0=gain_raw[:], scalar1=s_norm, scalar2=s_ffn, op0=ALU.mult, op1=ALU.mult
+                out=gain[:], in0=ln2_w_raw[:], scalar1=s_norm, scalar2=s_ffn, op0=ALU.mult, op1=ALU.mult
             )
             nc.vector.tensor_mul(out=s_ffn_sq[:], in0=s_ffn, in1=s_ffn)
 
         grouped = {}
         codes = {}
         scales = {}
-        acc = {}
+        product = {}
         v = {}
-        stats = {}
+        sums = {}
         normed = {}
-        turned = {}
 
         def transpose_h(i):
-            grouped[i] = front.tile([P, PASSES * P * 4], BF16, tag="grouped", name="h_grouped", align_bytes=64)
+            grouped[i] = front.tile([P, PASSES * P * PACK], BF16, tag="grouped", name="h_grouped", align_bytes=64)
             k_to_partitions(nc, psum, h_raw[i], ident, grouped[i], (nc.scalar.copy, nc.scalar.copy))
 
         def quantise_h(i):
             codes[i] = front.tile([P, PASSES * P], U32, tag="codes", name="h_codes", align_bytes=64)
             scales[i] = front.tile([P, PASSES * P], U8, tag="scales", name="h_scales", align_bytes=64)
+            words = PASSES * P // 2
             for half in range(2):
                 nc.vector.quantize_mx(
-                    out=codes[i][:, half * 2 * P : (half + 1) * 2 * P].bitcast(FP8X4),
-                    scales=scales[i][:, half * 2 * P : (half + 1) * 2 * P],
-                    in_=grouped[i][:, half * 8 * P : (half + 1) * 8 * P],
+                    out=codes[i][:, half * words : (half + 1) * words].bitcast(FP8X4),
+                    scales=scales[i][:, half * words : (half + 1) * words],
+                    in_=grouped[i][:, half * words * PACK : (half + 1) * words * PACK],
                 )
 
         def multiply(i):
-            acc[i] = psum.tile([P, CHANNELS], F32, tag="acc", name="acc")
+            product[i] = psum.tile([P, CHANNELS], F32, tag="product", name="product")
             for g in range(PASSES):
                 nc.tensor.matmul_mx(
-                    out=acc[i][:],
+                    out=product[i][:],
                     lhsT=codes[i][:, g * P : (g + 1) * P].bitcast(FP8X4),
                     lhsT_scale=scales[i][:, g * P : (g + 1) * P],
                     rhs=w_codes[:, g, :].bitcast(FP8X4),
@@ -158,16 +159,16 @@ def tile_transformerconvblock_pc_kernel(
         def add_bias(i):
             v[i] = back.tile([P, CHANNELS], F32, tag="v", name="v")
             nc.vector.tensor_tensor(
-                out=v[i][:], in0=acc[i][:], in1=bias_all[:].rearrange("p t r -> p (t r)"), op=ALU.add
+                out=v[i][:], in0=product[i][:], in1=bias_all[:].rearrange("p t r -> p (t r)"), op=ALU.add
             )
 
         def sum_up(i):
-            stats[i] = back.tile([P, 6], F32, tag="stats", name="stats")
-            nc.vector.bn_stats(out=stats[i][:], in_=v[i][:])
+            sums[i] = back.tile([P, 6], F32, tag="sums", name="sums")
+            nc.vector.bn_stats(out=sums[i][:], in_=v[i][:])
 
         def normalise(i):
             moments = back.tile([P, 2], F32, tag="moments")
-            nc.vector.bn_aggr(out=moments[:], in_=stats[i][:])
+            nc.vector.bn_aggr(out=moments[:], in_=sums[i][:])
             neg_mean = back.tile([P, 1], F32, tag="neg_mean")
             nc.gpsimd.tensor_scalar(
                 out=neg_mean[:], in0=moments[:, 0:1], scalar1=-1.0, scalar2=0.0, op0=ALU.mult, op1=ALU.add
@@ -181,10 +182,12 @@ def tile_transformerconvblock_pc_kernel(
                 out=normed[i][:], in0=v[i][:], scalar1=neg_mean[:], scalar2=inv_std[:], op0=ALU.add, op1=ALU.mult
             )
 
+        turned = {}
+
         def turn_back(b):
             turned[b] = [
-                psum.tile([P, 2, IMAGE_PIXELS], F32, tag="bank", name="turned%d" % half, bufs=TURN_BANKS)
-                for half in range(2)
+                psum.tile([P, 2, IMAGE_PIXELS], F32, tag="bank", name="turned%d" % bank_index, bufs=TURN_BANKS)
+                for bank_index in range(CH_BLOCKS // 2)
             ]
             for part in range(TILES_IMAGE):
                 for t in range(CH_BLOCKS):
@@ -202,7 +205,7 @@ def tile_transformerconvblock_pc_kernel(
                     out=summed[:, t, :],
                     in0=turned[b][t // 2][:, t % 2, :],
                     scalar=gain[:, t : t + 1],
-                    in1=x_raw[b][:, t * IMAGE_PIXELS : (t + 1) * IMAGE_PIXELS],
+                    in1=x_raw[:, b, t, :],
                     op0=ALU.mult,
                     op1=ALU.add,
                 )
@@ -210,9 +213,7 @@ def tile_transformerconvblock_pc_kernel(
                 nc.scalar.activation(
                     out=result[:, t, :], in_=summed[:, t, :], func=ACT.Relu, bias=shift[:, t : t + 1], scale=1.0
                 )
-                nc.sync.dma_start(
-                    out=out_images[:, b, t * IMAGE_PIXELS : (t + 1) * IMAGE_PIXELS], in_=result[:, t, :]
-                )
+                nc.sync.dma_start(out=out_blocks[:, b, t, :], in_=result[:, t, :])
 
         transpose_h(0)
         quantise_h(0)
@@ -220,20 +221,21 @@ def tile_transformerconvblock_pc_kernel(
         for i in range(1, AHEAD):
             transpose_h(i)
             quantise_h(i)
-        for i in range(TILES + BEHIND):
-            image_done = (i - BEHIND) // TILES_IMAGE if (i - BEHIND) % TILES_IMAGE == 0 else -1
+        for i in range(STEPS):
+            first_tile = i - BEHIND
+            image_due = first_tile // TILES_IMAGE if first_tile >= 0 and first_tile % TILES_IMAGE == 0 else None
             if i < TILES:
                 multiply(i)
             if i + AHEAD < TILES:
                 transpose_h(i + AHEAD)
-            if 0 <= image_done < IMAGES:
-                turn_back(image_done)
+            if image_due is not None:
+                turn_back(image_due)
             if i < TILES:
                 add_bias(i)
-            if 0 <= i - 1 < TILES:
+            if 1 <= i <= TILES:
                 normalise(i - 1)
-            if 0 <= image_done < IMAGES:
-                finish(image_done)
+            if image_due is not None:
+                finish(image_due)
             if i + AHEAD < TILES:
                 quantise_h(i + AHEAD)
             if i < TILES:
@@ -246,27 +248,20 @@ def load_rows(nc, pool, rows, name, pieces):
     for piece in range(pieces):
         part = pool.tile([P, width], BF16, name="%s_%d" % (name, piece))
         nc.sync.dma_start(out=part[:], in_=rows[:, piece * width : (piece + 1) * width])
-        for j in range(2 // pieces):
-            halves.append(part[:, j * (K // 2) : (j + 1) * (K // 2)])
+        for first in range(0, width, K_HALF):
+            halves.append(part[:, first : first + K_HALF])
     return halves
 
 
-def load_x(nc, pool, x_images, x_raw):
-    b = len(x_raw)
-    x_tile = pool.tile([P, CH_BLOCKS * IMAGE_PIXELS], BF16, name="x_raw%d" % b)
-    nc.sync.dma_start(out=x_tile[:], in_=x_images[:, b, :])
-    x_raw.append(x_tile)
-
-
-def k_to_partitions(nc, psum, rows, ident, grouped, copiers):
-    grouped_words = grouped[:].bitcast(F32).rearrange("p (g r u) -> p g r u", g=PASSES, u=2)
+def k_to_partitions(nc, psum, halves, ident, grouped, copiers):
+    grouped_pairs = grouped[:].bitcast(F32).rearrange("p (g r u) -> p g r u", g=PASSES, u=2)
     for half in range(2):
-        words = rows[half].bitcast(F32)
+        pairs = halves[half].bitcast(F32)
         bank = psum.tile([P, 2, 2, P], F32, tag="bank", bufs=TURN_BANKS)
-        for g in range(2):
+        for j in range(2):
             for u in range(2):
-                first = g * WORDS_PASS + u * P
-                nc.tensor.transpose(bank[:, g, u, :], words[:, first : first + P], ident[:])
+                first = j * PAIRS_PASS + u * P
+                nc.tensor.transpose(bank[:, j, u, :], pairs[:, first : first + P], ident[:])
         copiers[half](
-            out=grouped_words[:, 2 * half : 2 * half + 2, :, :], in_=bank[:].rearrange("p g u r -> p g r u")
+            out=grouped_pairs[:, 2 * half : 2 * half + 2, :, :], in_=bank[:].rearrange("p j u r -> p j r u")
         )

from contextlib import ExitStack

import concourse.mybir as mybir
from concourse.masks import make_identity

F32 = mybir.dt.float32
BF16 = mybir.dt.bfloat16
U32 = mybir.dt.uint32
U8 = mybir.dt.uint8
FP8X4 = mybir.dt.float8_e4m3fn_x4
ALU = mybir.AluOpType
ACT = mybir.ActivationFunctionType

P = 128
PACK = 4
K = 2048
K_PASS = P * PACK
PASSES = K // K_PASS
K_HALF = K // 2
PAIRS_PASS = K_PASS // 2
CHANNELS = 512
CH_BLOCKS = CHANNELS // P
IMAGES = 4
IMAGE_PIXELS = 256
TILES_IMAGE = IMAGE_PIXELS // P
TILES = IMAGES * TILES_IMAGE
EPS = 1e-5

MULT_COLS = 32
S_FFN_COL = 0
S_NORM_COL = 16

AHEAD = 2
BEHIND = 6
STEPS = (TILES - TILES_IMAGE) + BEHIND + 1
assert STEPS > TILES
PRODUCT_BANKS = 2
TURN_BANKS = 6

FLOPS = 2 * IMAGES * IMAGE_PIXELS * CHANNELS * K


def tile_transformerconvblock_pc_kernel(
    tc, h, ffn2_w, ffn2_b, scale_ffn, ln2_w, ln2_b, scale_norm2, x, out
):
    nc = tc.nc

    h_rows = h.rearrange("b i j k -> (b i j) k")
    w_blocks = ffn2_w.rearrange("(r t) k -> r t k", t=CH_BLOCKS)
    x_images = x.rearrange("b (r t) i j -> r b (t i j)", t=CH_BLOCKS)
    out_blocks = out.rearrange("b (r t) i j -> r b t (i j)", t=CH_BLOCKS)

    with ExitStack() as stack:
        stack.enter_context(tc.manual_schedule())
        const = stack.enter_context(tc.tile_pool(name="const", bufs=1))
        raw = stack.enter_context(tc.tile_pool(name="raw", bufs=1))
        front = stack.enter_context(tc.tile_pool(name="front", bufs=AHEAD + 1))
        back = stack.enter_context(tc.tile_pool(name="back", bufs=3))
        image = stack.enter_context(tc.tile_pool(name="image", bufs=3))
        psum = stack.enter_context(tc.psum_pool(name="psum", bufs=PRODUCT_BANKS))

        vec_rows = const.tile([P, CHANNELS + MULT_COLS], BF16)
        nc.vector.memset(vec_rows[:], 0.0)
        ones = const.tile([P, P], BF16)
        nc.vector.memset(ones[:], 1.0)
        nc.scalar.dma_start(out=vec_rows[0:1, 0:CHANNELS], in_=ffn2_b.rearrange("(o c) -> o c", o=1))
        for column, multiplier in ((S_FFN_COL, scale_ffn), (S_NORM_COL, scale_norm2)):
            nc.scalar.dma_start(
                out=vec_rows[0:1, CHANNELS + column : CHANNELS + column + 1],
                in_=multiplier.rearrange("(o c) -> o c", o=1),
            )
        ln2_w_raw = const.tile([P, CH_BLOCKS], BF16)
        nc.scalar.dma_start(out=ln2_w_raw[:], in_=ln2_w.rearrange("(r t) -> r t", t=CH_BLOCKS))
        ln2_b_raw = const.tile([P, CH_BLOCKS], BF16)
        nc.scalar.dma_start(out=ln2_b_raw[:], in_=ln2_b.rearrange("(r t) -> r t", t=CH_BLOCKS))

        table_warmer = const.tile([P, 1], F32)
        nc.scalar.activation(out=table_warmer[:], in_=ones[:, 0:1], func=ACT.Abs_reciprocal_sqrt)

        w_raw = [load_rows(nc, raw, w_blocks[:, t, :], "w_raw%d" % t, 1) for t in range(CH_BLOCKS)]
        h_raw = [load_rows(nc, raw, h_rows[i * P : (i + 1) * P, :], "h_raw%d" % i, 2) for i in range(TILES)]
        x_raw = raw.tile([P, IMAGES, CH_BLOCKS, IMAGE_PIXELS], BF16)
        nc.sync.dma_start(out=x_raw[:].rearrange("p b t c -> p b (t c)"), in_=x_images)

        ident = const.tile([P, P], F32)
        make_identity(nc, ident[:])

        w_codes = const.tile([P, PASSES, CHANNELS], U32, align_bytes=64)
        w_scales = const.tile([P, PASSES, CHANNELS], U8, align_bytes=64)
        for t in range(CH_BLOCKS):
            w_grouped = front.tile([P, PASSES * P * PACK], BF16, tag="grouped", align_bytes=64)
            k_to_partitions(nc, psum, w_raw[t], ident, w_grouped, (nc.scalar.copy, nc.vector.tensor_copy))
            for g in range(PASSES):
                nc.vector.quantize_mx(
                    out=w_codes[:, g, t * P : (t + 1) * P].bitcast(FP8X4),
                    scales=w_scales[:, g, t * P : (t + 1) * P],
                    in_=w_grouped[:, g * P * PACK : (g + 1) * P * PACK],
                )

        bias_all = const.tile([P, CH_BLOCKS, P], F32)
        mult = const.tile([P, MULT_COLS], F32)
        s_ffn = mult[:, S_FFN_COL : S_FFN_COL + 1]
        s_norm = mult[:, S_NORM_COL : S_NORM_COL + 1]
        s_ffn_sq = const.tile([P, 1], F32)
        eps = const.tile([P, 1], F32)
        gain = const.tile([P, CH_BLOCKS], F32)
        shift = const.tile([P, CH_BLOCKS], F32)

        def spread_constants():
            bias_ps = psum.tile([P, CHANNELS], F32, tag="bank", bufs=TURN_BANKS)
            nc.tensor.matmul(out=bias_ps[:], lhsT=ones[:], rhs=vec_rows[:, 0:CHANNELS], start=True, stop=True)
            mult_ps = psum.tile([P, MULT_COLS], F32, tag="bank", bufs=TURN_BANKS)
            nc.tensor.matmul(out=mult_ps[:], lhsT=ones[:], rhs=vec_rows[:, CHANNELS:], start=True, stop=True)
            nc.vector.tensor_copy(out=bias_all[:], in_=bias_ps[:].rearrange("p (r t) -> p t r", t=CH_BLOCKS))
            nc.vector.tensor_copy(out=mult[:], in_=mult_ps[:])
            nc.vector.tensor_scalar_mul(out=eps[:], in0=ones[:, 0:1], scalar1=EPS)
            nc.vector.tensor_scalar_mul(out=shift[:], in0=ln2_b_raw[:], scalar1=s_norm)
            nc.vector.tensor_scalar(
                out=gain[:], in0=ln2_w_raw[:], scalar1=s_norm, scalar2=s_ffn, op0=ALU.mult, op1=ALU.mult
            )
            nc.vector.tensor_mul(out=s_ffn_sq[:], in0=s_ffn, in1=s_ffn)

        grouped = {}
        codes = {}
        scales = {}
        product = {}
        v = {}
        sums = {}
        normed = {}

        def transpose_h(i):
            grouped[i] = front.tile([P, PASSES * P * PACK], BF16, tag="grouped", name="h_grouped", align_bytes=64)
            k_to_partitions(nc, psum, h_raw[i], ident, grouped[i], (nc.scalar.copy, nc.scalar.copy))

        def quantise_h(i):
            codes[i] = front.tile([P, PASSES * P], U32, tag="codes", name="h_codes", align_bytes=64)
            scales[i] = front.tile([P, PASSES * P], U8, tag="scales", name="h_scales", align_bytes=64)
            words = PASSES * P // 2
            for half in range(2):
                nc.vector.quantize_mx(
                    out=codes[i][:, half * words : (half + 1) * words].bitcast(FP8X4),
                    scales=scales[i][:, half * words : (half + 1) * words],
                    in_=grouped[i][:, half * words * PACK : (half + 1) * words * PACK],
                )

        def multiply(i):
            product[i] = psum.tile([P, CHANNELS], F32, tag="product", name="product")
            for g in range(PASSES):
                nc.tensor.matmul_mx(
                    out=product[i][:],
                    lhsT=codes[i][:, g * P : (g + 1) * P].bitcast(FP8X4),
                    lhsT_scale=scales[i][:, g * P : (g + 1) * P],
                    rhs=w_codes[:, g, :].bitcast(FP8X4),
                    rhs_scale=w_scales[:, g, :],
                    start=(g == 0),
                    stop=(g == PASSES - 1),
                )

        def add_bias(i):
            v[i] = back.tile([P, CHANNELS], F32, tag="v", name="v")
            nc.vector.tensor_tensor(
                out=v[i][:], in0=product[i][:], in1=bias_all[:].rearrange("p t r -> p (t r)"), op=ALU.add
            )

        def sum_up(i):
            sums[i] = back.tile([P, 6], F32, tag="sums", name="sums")
            nc.vector.bn_stats(out=sums[i][:], in_=v[i][:])

        def normalise(i):
            moments = back.tile([P, 2], F32, tag="moments")
            nc.vector.bn_aggr(out=moments[:], in_=sums[i][:])
            neg_mean = back.tile([P, 1], F32, tag="neg_mean")
            nc.gpsimd.tensor_scalar(
                out=neg_mean[:], in0=moments[:, 0:1], scalar1=-1.0, scalar2=0.0, op0=ALU.mult, op1=ALU.add
            )
            inv_std = back.tile([P, 1], F32, tag="inv_std")
            nc.scalar.activation(
                out=inv_std[:], in_=moments[:, 1:2], func=ACT.Abs_reciprocal_sqrt, bias=eps[:], scale=s_ffn_sq[:]
            )
            normed[i] = back.tile([P, CHANNELS], F32, tag="normed", name="normed", bufs=BEHIND + 1)
            nc.gpsimd.tensor_scalar(
                out=normed[i][:], in0=v[i][:], scalar1=neg_mean[:], scalar2=inv_std[:], op0=ALU.add, op1=ALU.mult
            )

        turned = {}

        def turn_back(b):
            turned[b] = [
                psum.tile([P, 2, IMAGE_PIXELS], F32, tag="bank", name="turned%d" % bank_index, bufs=TURN_BANKS)
                for bank_index in range(CH_BLOCKS // 2)
            ]
            for part in range(TILES_IMAGE):
                for t in range(CH_BLOCKS):
                    nc.tensor.transpose(
                        turned[b][t // 2][:, t % 2, part * P : (part + 1) * P],
                        normed[b * TILES_IMAGE + part][:, t * P : (t + 1) * P],
                        ident[:],
                    )

        def finish(b):
            summed = image.tile([P, CH_BLOCKS, IMAGE_PIXELS], F32, tag="summed")
            result = image.tile([P, CH_BLOCKS, IMAGE_PIXELS], F32, tag="result")
            for t in range(CH_BLOCKS):
                nc.vector.scalar_tensor_tensor(
                    out=summed[:, t, :],
                    in0=turned[b][t // 2][:, t % 2, :],
                    scalar=gain[:, t : t + 1],
                    in1=x_raw[:, b, t, :],
                    op0=ALU.mult,
                    op1=ALU.add,
                )
            for t in range(CH_BLOCKS):
                nc.scalar.activation(
                    out=result[:, t, :], in_=summed[:, t, :], func=ACT.Relu, bias=shift[:, t : t + 1], scale=1.0
                )
                nc.sync.dma_start(out=out_blocks[:, b, t, :], in_=result[:, t, :])

        transpose_h(0)
        quantise_h(0)
        spread_constants()
        for i in range(1, AHEAD):
            transpose_h(i)
            quantise_h(i)
        for i in range(STEPS):
            first_tile = i - BEHIND
            image_due = first_tile // TILES_IMAGE if first_tile >= 0 and first_tile % TILES_IMAGE == 0 else None
            if i < TILES:
                multiply(i)
            if i + AHEAD < TILES:
                transpose_h(i + AHEAD)
            if image_due is not None:
                turn_back(image_due)
            if i < TILES:
                add_bias(i)
            if 1 <= i <= TILES:
                normalise(i - 1)
            if image_due is not None:
                finish(image_due)
            if i + AHEAD < TILES:
                quantise_h(i + AHEAD)
            if i < TILES:
                sum_up(i)


def load_rows(nc, pool, rows, name, pieces):
    width = K // pieces
    halves = []
    for piece in range(pieces):
        part = pool.tile([P, width], BF16, name="%s_%d" % (name, piece))
        nc.sync.dma_start(out=part[:], in_=rows[:, piece * width : (piece + 1) * width])
        for first in range(0, width, K_HALF):
            halves.append(part[:, first : first + K_HALF])
    return halves


def k_to_partitions(nc, psum, halves, ident, grouped, copiers):
    grouped_pairs = grouped[:].bitcast(F32).rearrange("p (g r u) -> p g r u", g=PASSES, u=2)
    for half in range(2):
        pairs = halves[half].bitcast(F32)
        bank = psum.tile([P, 2, 2, P], F32, tag="bank", bufs=TURN_BANKS)
        for j in range(2):
            for u in range(2):
                first = j * PAIRS_PASS + u * P
                nc.tensor.transpose(bank[:, j, u, :], pairs[:, first : first + P], ident[:])
        copiers[half](
            out=grouped_pairs[:, 2 * half : 2 * half + 2, :, :], in_=bank[:].rearrange("p j u r -> p j r u")
        )
